import numpy as np
import ml_dtypes


def mxq(x, axis, fmt="e4m3"):
    dtype, down = {"e4m3": (ml_dtypes.float8_e4m3fn, 7), "e5m2": (ml_dtypes.float8_e5m2, 14)}[fmt]
    v = np.moveaxis(np.asarray(x, np.float32).astype(ml_dtypes.bfloat16).astype(np.float64), axis, -1)
    blocks = v.reshape(v.shape[:-1] + (-1, 32))
    amax = np.abs(blocks).max(-1, keepdims=True)
    byte = np.maximum(np.where(amax > 0, np.frexp(amax)[1] - 1 + 127, 0) - down, 1)
    scale = np.exp2(byte - 127.0)
    codes = (blocks / scale).astype(np.float32).astype(dtype).astype(np.float64)
    return np.moveaxis((codes * scale).reshape(v.shape), -1, axis)


WIDE = False


def mx_kscale(k):
    if not WIDE:
        return np.ones(k)
    levels = np.array([10, -10, 5, -5, 0])
    a = np.random.permutation(np.resize(levels, k // 512 * 4)).reshape(k // 512, 4)
    idx = np.arange(k)
    return np.exp2(a[idx // 512, idx % 128 // 32])


BF16 = ml_dtypes.bfloat16


def bf(x):
    return np.asarray(x, np.float32).astype(BF16)


def f64(x):
    return np.asarray(x).astype(np.float64)


N, K, C = 4096, 1024, 1024


def draw(rows, f, total):
    x = np.random.standard_normal((rows, f.size))
    for v in np.unique(f):
        m = f == v
        x[:, m] -= x[:, m].mean(1, keepdims=True)
    top = (f == f.max()).astype(np.float64)
    return np.sqrt(K / (2.0 * np.sqrt(C))) * x * f + total * np.random.standard_normal((rows, 1)) * top / top.sum()


def setup_inputs():
    s = mx_kscale(C)
    return {"output": bf(draw(N, s, 0.3 * K)), "code_book": bf(draw(K, 1.0 / s, 0.3 * K))}


def reference(output, code_book):
    output, code_book = f64(output), f64(code_book)
    K, C = code_book.shape
    dot = mxq(output, 1, "e4m3") @ mxq(code_book, 1, "e4m3").T
    o_sum = np.sum(output, axis=1, keepdims=True)
    c_sum = np.sum(code_book, axis=1)[None, :]
    return (2.0 * dot + float(C) - o_sum - c_sum) / float(K)

@@ -1,0 +1,213 @@
+from contextlib import ExitStack
+
+import concourse.mybir as mybir
+from concourse.masks import make_identity
+
+F32 = mybir.dt.float32
+BF16 = mybir.dt.bfloat16
+U32 = mybir.dt.uint32
+U8 = mybir.dt.uint8
+FP8X4 = mybir.dt.float8_e4m3fn_x4
+ALU = mybir.AluOpType
+ACT = mybir.ActivationFunctionType
+
+P = 128
+N_ROWS = 4096
+C_LEN = 1024
+N_CODES = 1024
+FLOPS = 2 * N_ROWS * C_LEN * N_CODES
+
+S_PER = 4
+N_BATCH = N_ROWS // (P * S_PER)
+JT = N_CODES // P
+PINNED = False
+V_OSUM = (3,)
+V_TX = ()
+
+
+def tile_codingclassifier_kernel(tc, output, code_book, out):
+    nc = tc.nc
+    with ExitStack() as ctx:
+        if PINNED:
+            ctx.enter_context(tc.manual_schedule())
+        const = ctx.enter_context(tc.tile_pool(name="const", bufs=1))
+        xin = ctx.enter_context(tc.tile_pool(name="xin", bufs=N_BATCH))
+        gpool = ctx.enter_context(tc.tile_pool(name="gpool", bufs=8))
+        qpool = ctx.enter_context(tc.tile_pool(name="qpool", bufs=10))
+        dpool = ctx.enter_context(tc.tile_pool(name="dpool", bufs=5))
+        rpool = ctx.enter_context(tc.tile_pool(name="rpool", bufs=6))
+        spool = ctx.enter_context(tc.tile_pool(name="spool", bufs=12))
+        jpool = ctx.enter_context(tc.tile_pool(name="jpool", bufs=1))
+        tpool = ctx.enter_context(tc.psum_pool(name="tpool", bufs=4))
+        apool = ctx.enter_context(tc.psum_pool(name="apool", bufs=4))
+
+        ident = const.tile([P, P], F32, name="ident")
+        make_identity(nc, ident[:])
+
+        cb_sb = const.tile([P, JT * C_LEN], BF16, name="cb_sb")
+        cb_view = code_book.rearrange("(t p) c -> p t c", p=P)
+        for a in range(4):
+            nc.sync.dma_start(
+                out=cb_sb[:, a * 2048 : (a + 1) * 2048].rearrange("p (t c) -> p t c", t=2),
+                in_=cb_view[:, 2 * a : 2 * a + 2, :],
+            )
+        x_view = output.rearrange("(b p s) c -> b p (s c)", p=P, s=S_PER)
+        o_view = out.rearrange("(b p s) j -> b p (s j)", p=P, s=S_PER)
+        x_tiles = []
+        for b in range(N_BATCH):
+            x_sb = xin.tile([P, S_PER * C_LEN], BF16, name="x_sb")
+            nc.sync.dma_start(out=x_sb[:], in_=x_view[b])
+            x_tiles.append(x_sb)
+
+        junk_v = jpool.tile([P, C_LEN], BF16, name="junk_v")
+        junk_s = jpool.tile([P, C_LEN], BF16, name="junk_s")
+
+        gcb = const.tile([P, 2 * N_CODES * 4], BF16, name="gcb", align_bytes=64)
+        gcb_w = gcb[:].bitcast(F32).rearrange("p (g j u) -> p g j u", g=2, u=2)
+        cb_w = cb_sb[:].bitcast(F32)
+        cbc = const.tile([P, 2 * N_CODES], U32, name="cbc", align_bytes=64)
+        cbs = const.tile([P, 2 * N_CODES], U8, name="cbs", align_bytes=64)
+        ncs = const.tile([P, JT], F32, name="ncs")
+        for t in range(JT):
+            tp = tpool.tile([P, 4, P], F32, name="tp")
+            for q in range(4):
+                nc.tensor.transpose(
+                    out=tp[:, q, :],
+                    in_=cb_w[:, t * 512 + q * P : t * 512 + (q + 1) * P],
+                    identity=ident[:],
+                )
+            src = tp[:].rearrange("p (g u) r -> p g r u", g=2)
+            dst = gcb_w[:, :, t * P : (t + 1) * P, :]
+            if t % 2 == 0:
+                nc.scalar.copy(out=dst, in_=src)
+            else:
+                nc.vector.tensor_copy(out=dst, in_=src)
+            nc.vector.tensor_scalar(
+                out=junk_v[:],
+                in0=cb_sb[:, t * C_LEN : (t + 1) * C_LEN],
+                scalar1=-1.0,
+                scalar2=None,
+                op0=ALU.mult,
+                op1=ALU.add,
+                accum_out=ncs[:, t : t + 1],
+            )
+            if t % 4 == 3:
+                for g in range(2):
+                    off = g * N_CODES + (t // 4) * 512
+                    nc.vector.quantize_mx(
+                        out=cbc[:, off : off + 512].bitcast(FP8X4),
+                        scales=cbs[:, off : off + 512],
+                        in_=gcb[:, off * 4 : (off + 512) * 4],
+                    )
+
+        tps = {}
+        xq = {}
+        dts = {}
+
+        def transposes(b):
+            xw = x_tiles[b][:].bitcast(F32)
+            for s in range(S_PER):
+                tp = tpool.tile([P, 4, P], F32, name="tp")
+                for q in range(4):
+                    nc.tensor.transpose(
+                        out=tp[:, q, :],
+                        in_=xw[:, s * 512 + q * P : s * 512 + (q + 1) * P],
+                        identity=ident[:],
+                    )
+                tps[(b, s)] = tp
+
+        def prepare(b, s):
+            i = (b * S_PER + s) % 8
+            grp = gpool.tile([P, C_LEN], BF16, name="grp", align_bytes=64)
+            dst = grp[:].bitcast(F32).rearrange("p (g r u) -> p g r u", g=2, u=2)
+            src = tps[(b, s)][:].rearrange("p (g u) r -> p g r u", g=2)
+            if i in V_TX:
+                nc.vector.tensor_copy(out=dst, in_=src)
+            else:
+                nc.scalar.copy(out=dst, in_=src)
+            nos = spool.tile([P, 1], F32, name="nos")
+            xrow = x_tiles[b][:, s * C_LEN : (s + 1) * C_LEN]
+            if i in V_OSUM:
+                nc.vector.tensor_scalar(
+                    out=junk_v[:], in0=xrow, scalar1=-1.0, scalar2=None,
+                    op0=ALU.mult, op1=ALU.add, accum_out=nos[:],
+                )
+            else:
+                nc.scalar.activation(
+                    out=junk_s[:], in_=xrow, func=ACT.Copy, scale=-1.0, accum_out=nos[:],
+                )
+            xc = qpool.tile([P, 256], U32, name="xc", align_bytes=64)
+            xs = qpool.tile([P, 256], U8, name="xs", align_bytes=64)
+            nc.vector.quantize_mx(out=xc[:].bitcast(FP8X4), scales=xs[:], in_=grp[:])
+            xq[(b, s)] = (xc, xs)
+            return nos
+
+        def dbuild(b, s, nos):
+            d = dpool.tile([P, N_CODES], F32, name="d")
+            nc.gpsimd.tensor_scalar(
+                out=d[:], in0=cc[:], scalar1=nos[:], scalar2=1.0 / 1024.0,
+                op0=ALU.add, op1=ALU.mult,
+            )
+            dts[(b, s)] = d
+
+        res_box = [None]
+
+        def multiply(b, s):
+            xc, xs = xq[(b, s)]
+            d = dts[(b, s)]
+            if s % 2 == 0:
+                res = rpool.tile([P, 2 * N_CODES], F32, name="res")
+                res_box[0] = res
+            res = res_box[0]
+            for h in range(2):
+                acc = apool.tile([P, 512], F32, name="acc")
+                for g in range(2):
+                    off = g * N_CODES + h * 512
+                    nc.tensor.matmul_mx(
+                        out=acc[:],
+                        lhsT=xc[:, g * P : (g + 1) * P].bitcast(FP8X4),
+                        lhsT_scale=xs[:, g * P : (g + 1) * P],
+                        rhs=cbc[:, off : off + 512].bitcast(FP8X4),
+                        rhs_scale=cbs[:, off : off + 512],
+                        start=(g == 0),
+                        stop=(g == 1),
+                    )
+                col = (s % 2) * N_CODES + h * 512
+                nc.vector.scalar_tensor_tensor(
+                    out=res[:, col : col + 512],
+                    in0=acc[:],
+                    scalar=2.0 / 1024.0,
+                    in1=d[:, h * 512 : (h + 1) * 512],
+                    op0=ALU.mult,
+                    op1=ALU.add,
+                )
+            if s % 2 == 1:
+                lo = (s - 1) * N_CODES
+                nc.sync.dma_start(out=o_view[b][:, lo : lo + 2 * N_CODES], in_=res[:])
+
+        transposes(0)
+        rep = const.tile([P, JT, P], F32, name="rep")
+        nc.gpsimd.tensor_scalar(
+            out=rep[:], in0=ncs[:].unsqueeze(2).to_broadcast([P, JT, P]),
+            scalar1=1.0, scalar2=1024.0, op0=ALU.mult, op1=ALU.add,
+        )
+        cc = const.tile([P, N_CODES], F32, name="cc")
+        for hh in range(2):
+            ccp = apool.tile([P, 512], F32, name="acc")
+            for t4 in range(4):
+                nc.tensor.transpose(
+                    out=ccp[:, t4 * P : (t4 + 1) * P], in_=rep[:, hh * 4 + t4, :], identity=ident[:]
+                )
+            nc.scalar.copy(out=cc[:, hh * 512 : (hh + 1) * 512], in_=ccp[:])
+        for s in range(S_PER):
+            nos = prepare(0, s)
+            dbuild(0, s, nos)
+
+        for b in range(N_BATCH):
+            if b + 1 < N_BATCH:
+                transposes(b + 1)
+            for s in range(S_PER):
+                multiply(b, s)
+                if b + 1 < N_BATCH:
+                    nos = prepare(b + 1, s)
+                    dbuild(b + 1, s, nos)

@@ -20,9 +20,7 @@ FLOPS = 2 * N_ROWS * C_LEN * N_CODES
 S_PER = 4
 N_BATCH = N_ROWS // (P * S_PER)
 JT = N_CODES // P
-PINNED = False
-V_OSUM = (3,)
-V_TX = ()
+PINNED = True
 
 
 def tile_codingclassifier_kernel(tc, output, code_book, out):
@@ -34,9 +32,9 @@ def tile_codingclassifier_kernel(tc, output, code_book, out):
         xin = ctx.enter_context(tc.tile_pool(name="xin", bufs=N_BATCH))
         gpool = ctx.enter_context(tc.tile_pool(name="gpool", bufs=8))
         qpool = ctx.enter_context(tc.tile_pool(name="qpool", bufs=10))
-        dpool = ctx.enter_context(tc.tile_pool(name="dpool", bufs=5))
+        dpool = ctx.enter_context(tc.tile_pool(name="dpool", bufs=6))
         rpool = ctx.enter_context(tc.tile_pool(name="rpool", bufs=6))
-        spool = ctx.enter_context(tc.tile_pool(name="spool", bufs=12))
+        spool = ctx.enter_context(tc.tile_pool(name="spool", bufs=14))
         jpool = ctx.enter_context(tc.tile_pool(name="jpool", bufs=1))
         tpool = ctx.enter_context(tc.psum_pool(name="tpool", bufs=4))
         apool = ctx.enter_context(tc.psum_pool(name="apool", bufs=4))
@@ -76,12 +74,10 @@ def tile_codingclassifier_kernel(tc, output, code_book, out):
                     in_=cb_w[:, t * 512 + q * P : t * 512 + (q + 1) * P],
                     identity=ident[:],
                 )
-            src = tp[:].rearrange("p (g u) r -> p g r u", g=2)
-            dst = gcb_w[:, :, t * P : (t + 1) * P, :]
-            if t % 2 == 0:
-                nc.scalar.copy(out=dst, in_=src)
-            else:
-                nc.vector.tensor_copy(out=dst, in_=src)
+            nc.scalar.copy(
+                out=gcb_w[:, :, t * P : (t + 1) * P, :],
+                in_=tp[:].rearrange("p (g u) r -> p g r u", g=2),
+            )
             nc.vector.tensor_scalar(
                 out=junk_v[:],
                 in0=cb_sb[:, t * C_LEN : (t + 1) * C_LEN],
@@ -101,7 +97,9 @@ def tile_codingclassifier_kernel(tc, output, code_book, out):
                     )
 
         tps = {}
+        grps = {}
         xq = {}
+        noss = {}
         dts = {}
 
         def transposes(b):
@@ -116,18 +114,18 @@ def tile_codingclassifier_kernel(tc, output, code_book, out):
                     )
                 tps[(b, s)] = tp
 
-        def prepare(b, s):
-            i = (b * S_PER + s) % 8
+        def copy_out(b, s):
             grp = gpool.tile([P, C_LEN], BF16, name="grp", align_bytes=64)
-            dst = grp[:].bitcast(F32).rearrange("p (g r u) -> p g r u", g=2, u=2)
-            src = tps[(b, s)][:].rearrange("p (g u) r -> p g r u", g=2)
-            if i in V_TX:
-                nc.vector.tensor_copy(out=dst, in_=src)
-            else:
-                nc.scalar.copy(out=dst, in_=src)
+            nc.scalar.copy(
+                out=grp[:].bitcast(F32).rearrange("p (g r u) -> p g r u", g=2, u=2),
+                in_=tps[(b, s)][:].rearrange("p (g u) r -> p g r u", g=2),
+            )
+            grps[(b, s)] = grp
+
+        def row_sum(b, s, on_vector):
             nos = spool.tile([P, 1], F32, name="nos")
             xrow = x_tiles[b][:, s * C_LEN : (s + 1) * C_LEN]
-            if i in V_OSUM:
+            if on_vector:
                 nc.vector.tensor_scalar(
                     out=junk_v[:], in0=xrow, scalar1=-1.0, scalar2=None,
                     op0=ALU.mult, op1=ALU.add, accum_out=nos[:],
@@ -136,16 +134,18 @@ def tile_codingclassifier_kernel(tc, output, code_book, out):
                 nc.scalar.activation(
                     out=junk_s[:], in_=xrow, func=ACT.Copy, scale=-1.0, accum_out=nos[:],
                 )
+            noss[(b, s)] = nos
+
+        def quantise(b, s):
             xc = qpool.tile([P, 256], U32, name="xc", align_bytes=64)
             xs = qpool.tile([P, 256], U8, name="xs", align_bytes=64)
-            nc.vector.quantize_mx(out=xc[:].bitcast(FP8X4), scales=xs[:], in_=grp[:])
+            nc.vector.quantize_mx(out=xc[:].bitcast(FP8X4), scales=xs[:], in_=grps[(b, s)][:])
             xq[(b, s)] = (xc, xs)
-            return nos
 
-        def dbuild(b, s, nos):
+        def dbuild(b, s):
             d = dpool.tile([P, N_CODES], F32, name="d")
             nc.gpsimd.tensor_scalar(
-                out=d[:], in0=cc[:], scalar1=nos[:], scalar2=1.0 / 1024.0,
+                out=d[:], in0=cc[:], scalar1=noss[(b, s)][:], scalar2=1.0 / 1024.0,
                 op0=ALU.add, op1=ALU.mult,
             )
             dts[(b, s)] = d
@@ -154,11 +154,7 @@ def tile_codingclassifier_kernel(tc, output, code_book, out):
 
         def multiply(b, s):
             xc, xs = xq[(b, s)]
-            d = dts[(b, s)]
-            if s % 2 == 0:
-                res = rpool.tile([P, 2 * N_CODES], F32, name="res")
-                res_box[0] = res
-            res = res_box[0]
+            accs = []
             for h in range(2):
                 acc = apool.tile([P, 512], F32, name="acc")
                 for g in range(2):
@@ -172,16 +168,33 @@ def tile_codingclassifier_kernel(tc, output, code_book, out):
                         start=(g == 0),
                         stop=(g == 1),
                     )
+                accs.append(acc)
+            return accs
+
+        def finish(b, s, accs):
+            d = dts[(b, s)]
+            last = b == N_BATCH - 1 and s >= 2
+            if s % 2 == 0:
+                res = rpool.tile([P, 2 * N_CODES], F32, name="res")
+                res_box[0] = res
+            res = res_box[0]
+            for h in range(2):
                 col = (s % 2) * N_CODES + h * 512
                 nc.vector.scalar_tensor_tensor(
                     out=res[:, col : col + 512],
-                    in0=acc[:],
+                    in0=accs[h][:],
                     scalar=2.0 / 1024.0,
                     in1=d[:, h * 512 : (h + 1) * 512],
                     op0=ALU.mult,
                     op1=ALU.add,
                 )
-            if s % 2 == 1:
+                if last and s == 3:
+                    lo = s * N_CODES + h * 512
+                    nc.sync.dma_start(out=o_view[b][:, lo : lo + 512], in_=res[:, col : col + 512])
+            if last and s == 2:
+                lo = s * N_CODES
+                nc.sync.dma_start(out=o_view[b][:, lo : lo + N_CODES], in_=res[:, 0:N_CODES])
+            if not last and s % 2 == 1:
                 lo = (s - 1) * N_CODES
                 nc.sync.dma_start(out=o_view[b][:, lo : lo + 2 * N_CODES], in_=res[:])
 
@@ -192,22 +205,49 @@ def tile_codingclassifier_kernel(tc, output, code_book, out):
             scalar1=1.0, scalar2=1024.0, op0=ALU.mult, op1=ALU.add,
         )
         cc = const.tile([P, N_CODES], F32, name="cc")
+        ccps = []
         for hh in range(2):
             ccp = apool.tile([P, 512], F32, name="acc")
             for t4 in range(4):
                 nc.tensor.transpose(
                     out=ccp[:, t4 * P : (t4 + 1) * P], in_=rep[:, hh * 4 + t4, :], identity=ident[:]
                 )
-            nc.scalar.copy(out=cc[:, hh * 512 : (hh + 1) * 512], in_=ccp[:])
+            ccps.append(ccp)
         for s in range(S_PER):
-            nos = prepare(0, s)
-            dbuild(0, s, nos)
+            copy_out(0, s)
+            row_sum(0, s, True)
+            quantise(0, s)
+        for hh in range(2):
+            nc.scalar.copy(out=cc[:, hh * 512 : (hh + 1) * 512], in_=ccps[hh][:])
+        for s in range(S_PER):
+            dbuild(0, s)
+        for s in range(S_PER):
+            row_sum(1, s, False)
 
-        for b in range(N_BATCH):
+        for s in range(S_PER):
+            if s == 2:
+                transposes(1)
+            accs = multiply(0, s)
+            if s >= 2:
+                copy_out(1, 2 * (s - 2))
+                copy_out(1, 2 * (s - 2) + 1)
+            finish(0, s, accs)
+            if s >= 2:
+                quantise(1, 2 * (s - 2))
+                quantise(1, 2 * (s - 2) + 1)
+            row_sum(2, s, False)
+            dbuild(1, s)
+
+        for b in range(1, N_BATCH):
             if b + 1 < N_BATCH:
                 transposes(b + 1)
             for s in range(S_PER):
-                multiply(b, s)
+                accs = multiply(b, s)
                 if b + 1 < N_BATCH:
-                    nos = prepare(b + 1, s)
-                    dbuild(b + 1, s, nos)
+                    copy_out(b + 1, s)
+                finish(b, s, accs)
+                if b + 1 < N_BATCH:
+                    quantise(b + 1, s)
+                    dbuild(b + 1, s)
+                if b + 2 < N_BATCH:
+                    row_sum(b + 2, s, False)

@@ -66,6 +66,28 @@ def tile_codingclassifier_kernel(tc, output, code_book, out):
         cbc = const.tile([P, 2 * N_CODES], U32, name="cbc", align_bytes=64)
         cbs = const.tile([P, 2 * N_CODES], U8, name="cbs", align_bytes=64)
         ncs = const.tile([P, JT], F32, name="ncs")
+        rep = const.tile([P, JT, P], F32, name="rep")
+        cc = const.tile([P, N_CODES], F32, name="cc")
+        ccps = []
+
+        def repeat_sums(hh):
+            nc.gpsimd.tensor_scalar(
+                out=rep[:, hh * 4 : (hh + 1) * 4, :],
+                in0=ncs[:, hh * 4 : (hh + 1) * 4].unsqueeze(2).to_broadcast([P, 4, P]),
+                scalar1=1.0, scalar2=1024.0, op0=ALU.mult, op1=ALU.add,
+            )
+
+        def spread_sums(hh):
+            ccp = apool.tile([P, 512], F32, name="acc")
+            for t4 in range(4):
+                nc.tensor.transpose(
+                    out=ccp[:, t4 * P : (t4 + 1) * P], in_=rep[:, hh * 4 + t4, :], identity=ident[:]
+                )
+            ccps.append(ccp)
+
+        def keep_sums(hh):
+            nc.scalar.copy(out=cc[:, hh * 512 : (hh + 1) * 512], in_=ccps[hh][:])
+
         for t in range(JT):
             tp = tpool.tile([P, 4, P], F32, name="tp")
             for q in range(4):
@@ -95,6 +117,10 @@ def tile_codingclassifier_kernel(tc, output, code_book, out):
                         scales=cbs[:, off : off + 512],
                         in_=gcb[:, off * 4 : (off + 512) * 4],
                     )
+                repeat_sums(t // 4)
+            if t == 5:
+                spread_sums(0)
+                keep_sums(0)
 
         tps = {}
         grps = {}
@@ -144,10 +170,13 @@ def tile_codingclassifier_kernel(tc, output, code_book, out):
 
         def dbuild(b, s):
             d = dpool.tile([P, N_CODES], F32, name="d")
-            nc.gpsimd.tensor_scalar(
-                out=d[:], in0=cc[:], scalar1=noss[(b, s)][:], scalar2=1.0 / 1024.0,
-                op0=ALU.add, op1=ALU.mult,
-            )
+            width = 512 if b == 0 else N_CODES
+            for lo in range(0, N_CODES, width):
+                nc.gpsimd.tensor_scalar(
+                    out=d[:, lo : lo + width], in0=cc[:, lo : lo + width],
+                    scalar1=noss[(b, s)][:], scalar2=1.0 / 1024.0,
+                    op0=ALU.add, op1=ALU.mult,
+                )
             dts[(b, s)] = d
 
         res_box = [None]
@@ -198,56 +227,50 @@ def tile_codingclassifier_kernel(tc, output, code_book, out):
                 lo = (s - 1) * N_CODES
                 nc.sync.dma_start(out=o_view[b][:, lo : lo + 2 * N_CODES], in_=res[:])
 
+        def on_vector(b, s):
+            return (b == 0 and s < 2) or (s == 3 and 1 <= b <= 4)
+
         transposes(0)
-        rep = const.tile([P, JT, P], F32, name="rep")
-        nc.gpsimd.tensor_scalar(
-            out=rep[:], in0=ncs[:].unsqueeze(2).to_broadcast([P, JT, P]),
-            scalar1=1.0, scalar2=1024.0, op0=ALU.mult, op1=ALU.add,
-        )
-        cc = const.tile([P, N_CODES], F32, name="cc")
-        ccps = []
-        for hh in range(2):
-            ccp = apool.tile([P, 512], F32, name="acc")
-            for t4 in range(4):
-                nc.tensor.transpose(
-                    out=ccp[:, t4 * P : (t4 + 1) * P], in_=rep[:, hh * 4 + t4, :], identity=ident[:]
-                )
-            ccps.append(ccp)
+        spread_sums(1)
         for s in range(S_PER):
             copy_out(0, s)
-            row_sum(0, s, True)
+        keep_sums(1)
+        for s in range(S_PER):
+            if not on_vector(0, s):
+                row_sum(0, s, False)
+        for s in range(S_PER):
             quantise(0, s)
-        for hh in range(2):
-            nc.scalar.copy(out=cc[:, hh * 512 : (hh + 1) * 512], in_=ccps[hh][:])
-        for s in range(S_PER):
+            if on_vector(0, s):
+                row_sum(0, s, True)
             dbuild(0, s)
-        for s in range(S_PER):
-            row_sum(1, s, False)
 
         for s in range(S_PER):
             if s == 2:
                 transposes(1)
             accs = multiply(0, s)
-            if s >= 2:
-                copy_out(1, 2 * (s - 2))
-                copy_out(1, 2 * (s - 2) + 1)
+            if s == 2:
+                for z in range(S_PER):
+                    copy_out(1, z)
+            row_sum(1, s, on_vector(1, s))
             finish(0, s, accs)
             if s >= 2:
                 quantise(1, 2 * (s - 2))
                 quantise(1, 2 * (s - 2) + 1)
-            row_sum(2, s, False)
             dbuild(1, s)
 
         for b in range(1, N_BATCH):
-            if b + 1 < N_BATCH:
+            more = b + 1 < N_BATCH
+            if more:
                 transposes(b + 1)
+                for z in range(S_PER):
+                    copy_out(b + 1, z)
             for s in range(S_PER):
                 accs = multiply(b, s)
-                if b + 1 < N_BATCH:
-                    copy_out(b + 1, s)
+                if more and not on_vector(b + 1, s):
+                    row_sum(b + 1, s, False)
                 finish(b, s, accs)
-                if b + 1 < N_BATCH:
+                if more:
                     quantise(b + 1, s)
+                    if on_vector(b + 1, s):
+                        row_sum(b + 1, s, True)
                     dbuild(b + 1, s)
-                if b + 2 < N_BATCH:
-                    row_sum(b + 2, s, False)

@@ -32,7 +32,6 @@ def tile_codingclassifier_kernel(tc, output, code_book, out):
         xin = ctx.enter_context(tc.tile_pool(name="xin", bufs=N_BATCH))
         gpool = ctx.enter_context(tc.tile_pool(name="gpool", bufs=8))
         qpool = ctx.enter_context(tc.tile_pool(name="qpool", bufs=10))
-        dpool = ctx.enter_context(tc.tile_pool(name="dpool", bufs=6))
         rpool = ctx.enter_context(tc.tile_pool(name="rpool", bufs=6))
         spool = ctx.enter_context(tc.tile_pool(name="spool", bufs=14))
         jpool = ctx.enter_context(tc.tile_pool(name="jpool", bufs=1))
@@ -58,11 +57,13 @@ def tile_codingclassifier_kernel(tc, output, code_book, out):
             x_tiles.append(x_sb)
 
         junk_v = jpool.tile([P, C_LEN], BF16, name="junk_v")
+        junk_w = jpool.tile([P, C_LEN // 2], F32, name="junk_w")
         junk_s = jpool.tile([P, C_LEN], BF16, name="junk_s")
 
         gcb = const.tile([P, 2 * N_CODES * 4], BF16, name="gcb", align_bytes=64)
         gcb_w = gcb[:].bitcast(F32).rearrange("p (g j u) -> p g j u", g=2, u=2)
-        cb_w = cb_sb[:].bitcast(F32)
+        cbz = const.tile([P, JT * C_LEN], BF16, name="cbz")
+        cb_w = cbz[:].bitcast(F32)
         cbc = const.tile([P, 2 * N_CODES], U32, name="cbc", align_bytes=64)
         cbs = const.tile([P, 2 * N_CODES], U8, name="cbs", align_bytes=64)
         ncs = const.tile([P, JT], F32, name="ncs")
@@ -74,7 +75,7 @@ def tile_codingclassifier_kernel(tc, output, code_book, out):
             nc.gpsimd.tensor_scalar(
                 out=rep[:, hh * 4 : (hh + 1) * 4, :],
                 in0=ncs[:, hh * 4 : (hh + 1) * 4].unsqueeze(2).to_broadcast([P, 4, P]),
-                scalar1=1.0, scalar2=1024.0, op0=ALU.mult, op1=ALU.add,
+                scalar1=-1.0 / 1024.0, scalar2=1.0, op0=ALU.mult, op1=ALU.add,
             )
 
         def spread_sums(hh):
@@ -89,6 +90,12 @@ def tile_codingclassifier_kernel(tc, output, code_book, out):
             nc.scalar.copy(out=cc[:, hh * 512 : (hh + 1) * 512], in_=ccps[hh][:])
 
         for t in range(JT):
+            if t % 2 == 0:
+                nc.vector.tensor_scalar(
+                    out=cbz[:, t * C_LEN : (t + 2) * C_LEN],
+                    in0=cb_sb[:, t * C_LEN : (t + 2) * C_LEN],
+                    scalar1=2.0 / 1024.0, scalar2=None, op0=ALU.mult,
+                )
             tp = tpool.tile([P, 4, P], F32, name="tp")
             for q in range(4):
                 nc.tensor.transpose(
@@ -100,11 +107,11 @@ def tile_codingclassifier_kernel(tc, output, code_book, out):
                 out=gcb_w[:, :, t * P : (t + 1) * P, :],
                 in_=tp[:].rearrange("p (g u) r -> p g r u", g=2),
             )
-            nc.vector.tensor_scalar(
-                out=junk_v[:],
-                in0=cb_sb[:, t * C_LEN : (t + 1) * C_LEN],
-                scalar1=-1.0,
-                scalar2=None,
+            nc.vector.scalar_tensor_tensor(
+                out=junk_w[:],
+                in0=cb_sb[:, t * C_LEN : t * C_LEN + 512],
+                scalar=1.0,
+                in1=cb_sb[:, t * C_LEN + 512 : (t + 1) * C_LEN],
                 op0=ALU.mult,
                 op1=ALU.add,
                 accum_out=ncs[:, t : t + 1],
@@ -126,7 +133,6 @@ def tile_codingclassifier_kernel(tc, output, code_book, out):
         grps = {}
         xq = {}
         noss = {}
-        dts = {}
 
         def transposes(b):
             xw = x_tiles[b][:].bitcast(F32)
@@ -153,12 +159,12 @@ def tile_codingclassifier_kernel(tc, output, code_book, out):
             xrow = x_tiles[b][:, s * C_LEN : (s + 1) * C_LEN]
             if on_vector:
                 nc.vector.tensor_scalar(
-                    out=junk_v[:], in0=xrow, scalar1=-1.0, scalar2=None,
+                    out=junk_v[:], in0=xrow, scalar1=-1.0 / 1024.0, scalar2=None,
                     op0=ALU.mult, op1=ALU.add, accum_out=nos[:],
                 )
             else:
                 nc.scalar.activation(
-                    out=junk_s[:], in_=xrow, func=ACT.Copy, scale=-1.0, accum_out=nos[:],
+                    out=junk_s[:], in_=xrow, func=ACT.Copy, scale=-1.0 / 1024.0, accum_out=nos[:],
                 )
             noss[(b, s)] = nos
 
@@ -167,17 +173,6 @@ def tile_codingclassifier_kernel(tc, output, code_book, out):
             xs = qpool.tile([P, 256], U8, name="xs", align_bytes=64)
             nc.vector.quantize_mx(out=xc[:].bitcast(FP8X4), scales=xs[:], in_=grps[(b, s)][:])
             xq[(b, s)] = (xc, xs)
-
-        def dbuild(b, s):
-            d = dpool.tile([P, N_CODES], F32, name="d")
-            width = 512 if b == 0 else N_CODES
-            for lo in range(0, N_CODES, width):
-                nc.gpsimd.tensor_scalar(
-                    out=d[:, lo : lo + width], in0=cc[:, lo : lo + width],
-                    scalar1=noss[(b, s)][:], scalar2=1.0 / 1024.0,
-                    op0=ALU.add, op1=ALU.mult,
-                )
-            dts[(b, s)] = d
 
         res_box = [None]
 
@@ -201,7 +196,6 @@ def tile_codingclassifier_kernel(tc, output, code_book, out):
             return accs
 
         def finish(b, s, accs):
-            d = dts[(b, s)]
             last = b == N_BATCH - 1 and s >= 2
             if s % 2 == 0:
                 res = rpool.tile([P, 2 * N_CODES], F32, name="res")
@@ -212,9 +206,9 @@ def tile_codingclassifier_kernel(tc, output, code_book, out):
                 nc.vector.scalar_tensor_tensor(
                     out=res[:, col : col + 512],
                     in0=accs[h][:],
-                    scalar=2.0 / 1024.0,
-                    in1=d[:, h * 512 : (h + 1) * 512],
-                    op0=ALU.mult,
+                    scalar=noss[(b, s)][:],
+                    in1=cc[:, h * 512 : (h + 1) * 512],
+                    op0=ALU.add,
                     op1=ALU.add,
                 )
                 if last and s == 3:
@@ -242,7 +236,6 @@ def tile_codingclassifier_kernel(tc, output, code_book, out):
             quantise(0, s)
             if on_vector(0, s):
                 row_sum(0, s, True)
-            dbuild(0, s)
 
         for s in range(S_PER):
             if s == 2:
@@ -256,7 +249,6 @@ def tile_codingclassifier_kernel(tc, output, code_book, out):
             if s >= 2:
                 quantise(1, 2 * (s - 2))
                 quantise(1, 2 * (s - 2) + 1)
-            dbuild(1, s)
 
         for b in range(1, N_BATCH):
             more = b + 1 < N_BATCH
@@ -273,4 +265,3 @@ def tile_codingclassifier_kernel(tc, output, code_book, out):
                     quantise(b + 1, s)
                     if on_vector(b + 1, s):
                         row_sum(b + 1, s, True)
-                    dbuild(b + 1, s)

@@ -20,26 +20,31 @@ FLOPS = 2 * N_ROWS * C_LEN * N_CODES
 S_PER = 4
 N_BATCH = N_ROWS // (P * S_PER)
 JT = N_CODES // P
-PINNED = True
+HALF = 512
+
+
+def on_vector(b, s):
+    return b == 0 or s == 3
 
 
 def tile_codingclassifier_kernel(tc, output, code_book, out):
     nc = tc.nc
     with ExitStack() as ctx:
-        if PINNED:
-            ctx.enter_context(tc.manual_schedule())
+        ctx.enter_context(tc.manual_schedule())
         const = ctx.enter_context(tc.tile_pool(name="const", bufs=1))
         xin = ctx.enter_context(tc.tile_pool(name="xin", bufs=N_BATCH))
-        gpool = ctx.enter_context(tc.tile_pool(name="gpool", bufs=8))
-        qpool = ctx.enter_context(tc.tile_pool(name="qpool", bufs=10))
+        gpool = ctx.enter_context(tc.tile_pool(name="gpool", bufs=3))
+        qpool = ctx.enter_context(tc.tile_pool(name="qpool", bufs=3))
         rpool = ctx.enter_context(tc.tile_pool(name="rpool", bufs=6))
-        spool = ctx.enter_context(tc.tile_pool(name="spool", bufs=14))
+        spool = ctx.enter_context(tc.tile_pool(name="spool", bufs=16))
         jpool = ctx.enter_context(tc.tile_pool(name="jpool", bufs=1))
         tpool = ctx.enter_context(tc.psum_pool(name="tpool", bufs=4))
         apool = ctx.enter_context(tc.psum_pool(name="apool", bufs=4))
 
         ident = const.tile([P, P], F32, name="ident")
         make_identity(nc, ident[:])
+        negh = const.tile([P, P], BF16, name="negh")
+        nc.gpsimd.memset(negh[:], -0.5)
 
         cb_sb = const.tile([P, JT * C_LEN], BF16, name="cb_sb")
         cb_view = code_book.rearrange("(t p) c -> p t c", p=P)
@@ -56,46 +61,27 @@ def tile_codingclassifier_kernel(tc, output, code_book, out):
             nc.sync.dma_start(out=x_sb[:], in_=x_view[b])
             x_tiles.append(x_sb)
 
-        junk_v = jpool.tile([P, C_LEN], BF16, name="junk_v")
-        junk_w = jpool.tile([P, C_LEN // 2], F32, name="junk_w")
         junk_s = jpool.tile([P, C_LEN], BF16, name="junk_s")
+        junk_w = jpool.tile([P, HALF], F32, name="junk_w")
 
-        gcb = const.tile([P, 2 * N_CODES * 4], BF16, name="gcb", align_bytes=64)
-        gcb_w = gcb[:].bitcast(F32).rearrange("p (g j u) -> p g j u", g=2, u=2)
         cbz = const.tile([P, JT * C_LEN], BF16, name="cbz")
         cb_w = cbz[:].bitcast(F32)
+        gcb = const.tile([P, 2 * N_CODES * 4], BF16, name="gcb", align_bytes=64)
+        gcb_w = gcb[:].bitcast(F32).rearrange("p (g j u) -> p g j u", g=2, u=2)
+        gcb_e = gcb[:].rearrange("p (g j e) -> p g j e", g=2, e=4)
         cbc = const.tile([P, 2 * N_CODES], U32, name="cbc", align_bytes=64)
         cbs = const.tile([P, 2 * N_CODES], U8, name="cbs", align_bytes=64)
-        ncs = const.tile([P, JT], F32, name="ncs")
-        rep = const.tile([P, JT, P], F32, name="rep")
         cc = const.tile([P, N_CODES], F32, name="cc")
-        ccps = []
+        ccps = {}
 
-        def repeat_sums(hh):
-            nc.gpsimd.tensor_scalar(
-                out=rep[:, hh * 4 : (hh + 1) * 4, :],
-                in0=ncs[:, hh * 4 : (hh + 1) * 4].unsqueeze(2).to_broadcast([P, 4, P]),
-                scalar1=-1.0 / 1024.0, scalar2=1.0, op0=ALU.mult, op1=ALU.add,
+        def scale_book(a):
+            nc.vector.tensor_scalar(
+                out=cbz[:, a * 2048 : (a + 1) * 2048],
+                in0=cb_sb[:, a * 2048 : (a + 1) * 2048],
+                scalar1=2.0 / 1024.0, scalar2=None, op0=ALU.mult,
             )
 
-        def spread_sums(hh):
-            ccp = apool.tile([P, 512], F32, name="acc")
-            for t4 in range(4):
-                nc.tensor.transpose(
-                    out=ccp[:, t4 * P : (t4 + 1) * P], in_=rep[:, hh * 4 + t4, :], identity=ident[:]
-                )
-            ccps.append(ccp)
-
-        def keep_sums(hh):
-            nc.scalar.copy(out=cc[:, hh * 512 : (hh + 1) * 512], in_=ccps[hh][:])
-
-        for t in range(JT):
-            if t % 2 == 0:
-                nc.vector.tensor_scalar(
-                    out=cbz[:, t * C_LEN : (t + 2) * C_LEN],
-                    in0=cb_sb[:, t * C_LEN : (t + 2) * C_LEN],
-                    scalar1=2.0 / 1024.0, scalar2=None, op0=ALU.mult,
-                )
+        def turn_book(t):
             tp = tpool.tile([P, 4, P], F32, name="tp")
             for q in range(4):
                 nc.tensor.transpose(
@@ -107,27 +93,32 @@ def tile_codingclassifier_kernel(tc, output, code_book, out):
                 out=gcb_w[:, :, t * P : (t + 1) * P, :],
                 in_=tp[:].rearrange("p (g u) r -> p g r u", g=2),
             )
-            nc.vector.scalar_tensor_tensor(
-                out=junk_w[:],
-                in0=cb_sb[:, t * C_LEN : t * C_LEN + 512],
-                scalar=1.0,
-                in1=cb_sb[:, t * C_LEN + 512 : (t + 1) * C_LEN],
-                op0=ALU.mult,
-                op1=ALU.add,
-                accum_out=ncs[:, t : t + 1],
+
+        def quantise_book(hh):
+            for g in range(2):
+                off = g * N_CODES + hh * HALF
+                nc.vector.quantize_mx(
+                    out=cbc[:, off : off + HALF].bitcast(FP8X4),
+                    scales=cbs[:, off : off + HALF],
+                    in_=gcb[:, off * 4 : (off + HALF) * 4],
+                )
+
+        def sum_book(hh):
+            ccp = apool.tile([P, HALF], F32, name="acc")
+            for i in range(8):
+                nc.tensor.matmul(
+                    out=ccp[:],
+                    lhsT=negh[:],
+                    rhs=gcb_e[:, i // 4, hh * HALF : (hh + 1) * HALF, i % 4],
+                    start=(i == 0),
+                    stop=(i == 7),
+                )
+            ccps[hh] = ccp
+
+        def keep_sums(hh):
+            nc.scalar.activation(
+                out=cc[:, hh * HALF : (hh + 1) * HALF], in_=ccps[hh][:], func=ACT.Copy, bias=1.0, scale=1.0,
             )
-            if t % 4 == 3:
-                for g in range(2):
-                    off = g * N_CODES + (t // 4) * 512
-                    nc.vector.quantize_mx(
-                        out=cbc[:, off : off + 512].bitcast(FP8X4),
-                        scales=cbs[:, off : off + 512],
-                        in_=gcb[:, off * 4 : (off + 512) * 4],
-                    )
-                repeat_sums(t // 4)
-            if t == 5:
-                spread_sums(0)
-                keep_sums(0)
 
         tps = {}
         grps = {}
@@ -147,48 +138,58 @@ def tile_codingclassifier_kernel(tc, output, code_book, out):
                 tps[(b, s)] = tp
 
         def copy_out(b, s):
-            grp = gpool.tile([P, C_LEN], BF16, name="grp", align_bytes=64)
+            if s == 0:
+                grp = gpool.tile([P, S_PER * C_LEN], BF16, name="grp", align_bytes=64)
+                grps[b] = grp
             nc.scalar.copy(
-                out=grp[:].bitcast(F32).rearrange("p (g r u) -> p g r u", g=2, u=2),
+                out=grps[b][:, s * C_LEN : (s + 1) * C_LEN].bitcast(F32).rearrange("p (g r u) -> p g r u", g=2, u=2),
                 in_=tps[(b, s)][:].rearrange("p (g u) r -> p g r u", g=2),
             )
-            grps[(b, s)] = grp
 
-        def row_sum(b, s, on_vector):
+        def row_sum(b, s):
             nos = spool.tile([P, 1], F32, name="nos")
-            xrow = x_tiles[b][:, s * C_LEN : (s + 1) * C_LEN]
-            if on_vector:
-                nc.vector.tensor_scalar(
-                    out=junk_v[:], in0=xrow, scalar1=-1.0 / 1024.0, scalar2=None,
-                    op0=ALU.mult, op1=ALU.add, accum_out=nos[:],
+            lo = s * C_LEN
+            if on_vector(b, s):
+                raw = spool.tile([P, 1], F32, name="raw")
+                nc.vector.scalar_tensor_tensor(
+                    out=junk_w[:],
+                    in0=x_tiles[b][:, lo : lo + HALF],
+                    scalar=1.0,
+                    in1=x_tiles[b][:, lo + HALF : lo + C_LEN],
+                    op0=ALU.mult, op1=ALU.add, accum_out=raw[:],
+                )
+                nc.gpsimd.tensor_scalar(
+                    out=nos[:], in0=raw[:], scalar1=-1.0 / 1024.0, scalar2=0.0, op0=ALU.mult, op1=ALU.add,
                 )
             else:
                 nc.scalar.activation(
-                    out=junk_s[:], in_=xrow, func=ACT.Copy, scale=-1.0 / 1024.0, accum_out=nos[:],
+                    out=junk_s[:], in_=x_tiles[b][:, lo : lo + C_LEN], func=ACT.Copy,
+                    scale=-1.0 / 1024.0, accum_out=nos[:],
                 )
             noss[(b, s)] = nos
 
-        def quantise(b, s):
-            xc = qpool.tile([P, 256], U32, name="xc", align_bytes=64)
-            xs = qpool.tile([P, 256], U8, name="xs", align_bytes=64)
-            nc.vector.quantize_mx(out=xc[:].bitcast(FP8X4), scales=xs[:], in_=grps[(b, s)][:])
-            xq[(b, s)] = (xc, xs)
+        def quantise(b):
+            xc = qpool.tile([P, S_PER * 256], U32, name="xc", align_bytes=64)
+            xs = qpool.tile([P, S_PER * 256], U8, name="xs", align_bytes=64)
+            nc.vector.quantize_mx(out=xc[:].bitcast(FP8X4), scales=xs[:], in_=grps[b][:])
+            xq[b] = (xc, xs)
 
         res_box = [None]
 
         def multiply(b, s):
-            xc, xs = xq[(b, s)]
+            xc, xs = xq[b]
             accs = []
             for h in range(2):
-                acc = apool.tile([P, 512], F32, name="acc")
+                acc = apool.tile([P, HALF], F32, name="acc")
                 for g in range(2):
-                    off = g * N_CODES + h * 512
+                    off = g * N_CODES + h * HALF
+                    col = s * 256 + g * P
                     nc.tensor.matmul_mx(
                         out=acc[:],
-                        lhsT=xc[:, g * P : (g + 1) * P].bitcast(FP8X4),
-                        lhsT_scale=xs[:, g * P : (g + 1) * P],
-                        rhs=cbc[:, off : off + 512].bitcast(FP8X4),
-                        rhs_scale=cbs[:, off : off + 512],
+                        lhsT=xc[:, col : col + P].bitcast(FP8X4),
+                        lhsT_scale=xs[:, col : col + P],
+                        rhs=cbc[:, off : off + HALF].bitcast(FP8X4),
+                        rhs_scale=cbs[:, off : off + HALF],
                         start=(g == 0),
                         stop=(g == 1),
                     )
@@ -202,18 +203,18 @@ def tile_codingclassifier_kernel(tc, output, code_book, out):
                 res_box[0] = res
             res = res_box[0]
             for h in range(2):
-                col = (s % 2) * N_CODES + h * 512
+                col = (s % 2) * N_CODES + h * HALF
                 nc.vector.scalar_tensor_tensor(
-                    out=res[:, col : col + 512],
+                    out=res[:, col : col + HALF],
                     in0=accs[h][:],
                     scalar=noss[(b, s)][:],
-                    in1=cc[:, h * 512 : (h + 1) * 512],
+                    in1=cc[:, h * HALF : (h + 1) * HALF],
                     op0=ALU.add,
                     op1=ALU.add,
                 )
                 if last and s == 3:
-                    lo = s * N_CODES + h * 512
-                    nc.sync.dma_start(out=o_view[b][:, lo : lo + 512], in_=res[:, col : col + 512])
+                    lo = s * N_CODES + h * HALF
+                    nc.sync.dma_start(out=o_view[b][:, lo : lo + HALF], in_=res[:, col : col + HALF])
             if last and s == 2:
                 lo = s * N_CODES
                 nc.sync.dma_start(out=o_view[b][:, lo : lo + N_CODES], in_=res[:, 0:N_CODES])
@@ -221,47 +222,38 @@ def tile_codingclassifier_kernel(tc, output, code_book, out):
                 lo = (s - 1) * N_CODES
                 nc.sync.dma_start(out=o_view[b][:, lo : lo + 2 * N_CODES], in_=res[:])
 
-        def on_vector(b, s):
-            return (b == 0 and s < 2) or (s == 3 and 1 <= b <= 4)
-
+        for a in range(4):
+            scale_book(a)
+        for t in range(JT):
+            turn_book(t)
+            if t == 3:
+                quantise_book(0)
+                row_sum(0, 0)
+                row_sum(0, 1)
+        quantise_book(1)
+        row_sum(0, 2)
+        sum_book(0)
+        keep_sums(0)
         transposes(0)
-        spread_sums(1)
         for s in range(S_PER):
             copy_out(0, s)
+        sum_book(1)
         keep_sums(1)
-        for s in range(S_PER):
-            if not on_vector(0, s):
-                row_sum(0, s, False)
-        for s in range(S_PER):
-            quantise(0, s)
-            if on_vector(0, s):
-                row_sum(0, s, True)
+        quantise(0)
+        row_sum(0, 3)
 
-        for s in range(S_PER):
-            if s == 2:
-                transposes(1)
-            accs = multiply(0, s)
-            if s == 2:
-                for z in range(S_PER):
-                    copy_out(1, z)
-            row_sum(1, s, on_vector(1, s))
-            finish(0, s, accs)
-            if s >= 2:
-                quantise(1, 2 * (s - 2))
-                quantise(1, 2 * (s - 2) + 1)
-
-        for b in range(1, N_BATCH):
+        for b in range(N_BATCH):
             more = b + 1 < N_BATCH
             if more:
                 transposes(b + 1)
-                for z in range(S_PER):
-                    copy_out(b + 1, z)
+                for s in range(S_PER):
+                    copy_out(b + 1, s)
             for s in range(S_PER):
                 accs = multiply(b, s)
                 if more and not on_vector(b + 1, s):
-                    row_sum(b + 1, s, False)
+                    row_sum(b + 1, s)
                 finish(b, s, accs)
-                if more:
-                    quantise(b + 1, s)
-                    if on_vector(b + 1, s):
-                        row_sum(b + 1, s, True)
+                if more and s == 1:
+                    quantise(b + 1)
+                if more and on_vector(b + 1, s):
+                    row_sum(b + 1, s)

@@ -45,6 +45,15 @@ def tile_codingclassifier_kernel(tc, output, code_book, out):
         make_identity(nc, ident[:])
         negh = const.tile([P, P], BF16, name="negh")
         nc.gpsimd.memset(negh[:], -0.5)
+        zeros = const.tile([P, HALF], BF16, name="zeros")
+        nc.vector.memset(zeros[:], 0.0)
+
+        def warm(n):
+            idle = apool.tile([P, HALF], F32, name="acc")
+            for rep_i in range(n):
+                nc.tensor.matmul(out=idle[:], lhsT=negh[:], rhs=zeros[:], start=True, stop=True)
+
+        warm(6)
 
         cb_sb = const.tile([P, JT * C_LEN], BF16, name="cb_sb")
         cb_view = code_book.rearrange("(t p) c -> p t c", p=P)
@@ -103,17 +112,19 @@ def tile_codingclassifier_kernel(tc, output, code_book, out):
                     in_=gcb[:, off * 4 : (off + HALF) * 4],
                 )
 
-        def sum_book(hh):
-            ccp = apool.tile([P, HALF], F32, name="acc")
+        def sum_book(a):
+            if a % 2 == 0:
+                ccp = apool.tile([P, HALF], F32, name="acc")
+                ccps[a // 2] = ccp
+            ccp = ccps[a // 2]
             for i in range(8):
                 nc.tensor.matmul(
-                    out=ccp[:],
+                    out=ccp[:, (a % 2) * 256 : (a % 2 + 1) * 256],
                     lhsT=negh[:],
-                    rhs=gcb_e[:, i // 4, hh * HALF : (hh + 1) * HALF, i % 4],
+                    rhs=gcb_e[:, i // 4, a * 256 : (a + 1) * 256, i % 4],
                     start=(i == 0),
                     stop=(i == 7),
                 )
-            ccps[hh] = ccp
 
         def keep_sums(hh):
             nc.scalar.activation(
@@ -224,20 +235,28 @@ def tile_codingclassifier_kernel(tc, output, code_book, out):
 
         for a in range(4):
             scale_book(a)
-        for t in range(JT):
-            turn_book(t)
-            if t == 3:
-                quantise_book(0)
-                row_sum(0, 0)
-                row_sum(0, 1)
+        turn_book(0)
+        turn_book(1)
+        warm(2)
+        turn_book(2)
+        turn_book(3)
+        quantise_book(0)
+        row_sum(0, 0)
+        row_sum(0, 1)
+        sum_book(0)
+        turn_book(4)
+        turn_book(5)
+        sum_book(1)
+        keep_sums(0)
+        turn_book(6)
+        turn_book(7)
         quantise_book(1)
         row_sum(0, 2)
-        sum_book(0)
-        keep_sums(0)
         transposes(0)
         for s in range(S_PER):
             copy_out(0, s)
-        sum_book(1)
+        sum_book(2)
+        sum_book(3)
         keep_sums(1)
         quantise(0)
         row_sum(0, 3)

@@ -24,7 +24,11 @@ HALF = 512
 
 
 def on_vector(b, s):
-    return b == 0 or s == 3
+    return b == 0
+
+
+def folded(b, s):
+    return b > 0 and s < 3
 
 
 def tile_codingclassifier_kernel(tc, output, code_book, out):
@@ -38,6 +42,7 @@ def tile_codingclassifier_kernel(tc, output, code_book, out):
         rpool = ctx.enter_context(tc.tile_pool(name="rpool", bufs=6))
         spool = ctx.enter_context(tc.tile_pool(name="spool", bufs=16))
         jpool = ctx.enter_context(tc.tile_pool(name="jpool", bufs=1))
+        fpool = ctx.enter_context(tc.tile_pool(name="fpool", bufs=6))
         tpool = ctx.enter_context(tc.psum_pool(name="tpool", bufs=4))
         apool = ctx.enter_context(tc.psum_pool(name="apool", bufs=4))
 
@@ -45,19 +50,12 @@ def tile_codingclassifier_kernel(tc, output, code_book, out):
         make_identity(nc, ident[:])
         negh = const.tile([P, P], BF16, name="negh")
         nc.gpsimd.memset(negh[:], -0.5)
-        zeros = const.tile([P, HALF], BF16, name="zeros")
-        nc.vector.memset(zeros[:], 0.0)
-
-        def warm(n):
-            idle = apool.tile([P, HALF], F32, name="acc")
-            for rep_i in range(n):
-                nc.tensor.matmul(out=idle[:], lhsT=negh[:], rhs=zeros[:], start=True, stop=True)
-
-        warm(6)
 
         cb_sb = const.tile([P, JT * C_LEN], BF16, name="cb_sb")
         cb_view = code_book.rearrange("(t p) c -> p t c", p=P)
-        for a in range(4):
+        for t in range(2):
+            nc.sync.dma_start(out=cb_sb[:, t * C_LEN : (t + 1) * C_LEN], in_=cb_view[:, t, :])
+        for a in range(1, 4):
             nc.sync.dma_start(
                 out=cb_sb[:, a * 2048 : (a + 1) * 2048].rearrange("p (t c) -> p t c", t=2),
                 in_=cb_view[:, 2 * a : 2 * a + 2, :],
@@ -83,10 +81,10 @@ def tile_codingclassifier_kernel(tc, output, code_book, out):
         cc = const.tile([P, N_CODES], F32, name="cc")
         ccps = {}
 
-        def scale_book(a):
+        def scale_book(lo, hi):
             nc.vector.tensor_scalar(
-                out=cbz[:, a * 2048 : (a + 1) * 2048],
-                in0=cb_sb[:, a * 2048 : (a + 1) * 2048],
+                out=cbz[:, lo * C_LEN : hi * C_LEN],
+                in0=cb_sb[:, lo * C_LEN : hi * C_LEN],
                 scalar1=2.0 / 1024.0, scalar2=None, op0=ALU.mult,
             )
 
@@ -157,6 +155,24 @@ def tile_codingclassifier_kernel(tc, output, code_book, out):
                 in_=tps[(b, s)][:].rearrange("p (g u) r -> p g r u", g=2),
             )
 
+        folds = {}
+        gate = const.tile([P, 8], U32, name="gate")
+
+        def fold_batch(b):
+            nc.gpsimd.tensor_copy(out=gate[:], in_=xq[b - 1][0][:, 0:8])
+            for s in range(S_PER):
+                if folded(b, s):
+                    lo = s * C_LEN
+                    fo = fpool.tile([P, HALF], F32, name="fo")
+                    nc.gpsimd.tensor_tensor(
+                        out=fo[:], in0=x_tiles[b][:, lo : lo + HALF], in1=x_tiles[b][:, lo + HALF : lo + C_LEN], op=ALU.add,
+                    )
+                    folds[(b, s)] = fo
+            xc = qpool.tile([P, S_PER * 256], U32, name="xc", align_bytes=64)
+            xs = qpool.tile([P, S_PER * 256], U8, name="xs", align_bytes=64)
+            nc.gpsimd.memset(xs[:, 0:64], 0)
+            xq[b] = (xc, xs)
+
         def row_sum(b, s):
             nos = spool.tile([P, 1], F32, name="nos")
             lo = s * C_LEN
@@ -172,6 +188,11 @@ def tile_codingclassifier_kernel(tc, output, code_book, out):
                 nc.gpsimd.tensor_scalar(
                     out=nos[:], in0=raw[:], scalar1=-1.0 / 1024.0, scalar2=0.0, op0=ALU.mult, op1=ALU.add,
                 )
+            elif folded(b, s):
+                nc.scalar.activation(
+                    out=junk_s[:, 0:HALF], in_=folds[(b, s)][:], func=ACT.Copy,
+                    scale=-1.0 / 1024.0, accum_out=nos[:],
+                )
             else:
                 nc.scalar.activation(
                     out=junk_s[:], in_=x_tiles[b][:, lo : lo + C_LEN], func=ACT.Copy,
@@ -179,11 +200,18 @@ def tile_codingclassifier_kernel(tc, output, code_book, out):
                 )
             noss[(b, s)] = nos
 
-        def quantise(b):
-            xc = qpool.tile([P, S_PER * 256], U32, name="xc", align_bytes=64)
-            xs = qpool.tile([P, S_PER * 256], U8, name="xs", align_bytes=64)
-            nc.vector.quantize_mx(out=xc[:].bitcast(FP8X4), scales=xs[:], in_=grps[b][:])
-            xq[b] = (xc, xs)
+        def quantise(b, parts=1):
+            if b == 0:
+                xc = qpool.tile([P, S_PER * 256], U32, name="xc", align_bytes=64)
+                xs = qpool.tile([P, S_PER * 256], U8, name="xs", align_bytes=64)
+                xq[b] = (xc, xs)
+            xc, xs = xq[b]
+            w = S_PER * 256 // parts
+            for i in range(parts):
+                nc.vector.quantize_mx(
+                    out=xc[:, i * w : (i + 1) * w].bitcast(FP8X4), scales=xs[:, i * w : (i + 1) * w],
+                    in_=grps[b][:, i * w * 4 : (i + 1) * w * 4],
+                )
 
         res_box = [None]
 
@@ -208,7 +236,7 @@ def tile_codingclassifier_kernel(tc, output, code_book, out):
             return accs
 
         def finish(b, s, accs):
-            last = b == N_BATCH - 1 and s >= 2
+            fine = 0 if b < N_BATCH - 2 else (2 if (b == N_BATCH - 1 and s >= 2) else 1)
             if s % 2 == 0:
                 res = rpool.tile([P, 2 * N_CODES], F32, name="res")
                 res_box[0] = res
@@ -223,21 +251,23 @@ def tile_codingclassifier_kernel(tc, output, code_book, out):
                     op0=ALU.add,
                     op1=ALU.add,
                 )
-                if last and s == 3:
+                if fine == 2:
                     lo = s * N_CODES + h * HALF
                     nc.sync.dma_start(out=o_view[b][:, lo : lo + HALF], in_=res[:, col : col + HALF])
-            if last and s == 2:
+            if fine == 1:
                 lo = s * N_CODES
-                nc.sync.dma_start(out=o_view[b][:, lo : lo + N_CODES], in_=res[:, 0:N_CODES])
-            if not last and s % 2 == 1:
+                col = (s % 2) * N_CODES
+                nc.sync.dma_start(out=o_view[b][:, lo : lo + N_CODES], in_=res[:, col : col + N_CODES])
+            if fine == 0 and s % 2 == 1:
                 lo = (s - 1) * N_CODES
                 nc.sync.dma_start(out=o_view[b][:, lo : lo + 2 * N_CODES], in_=res[:])
 
-        for a in range(4):
-            scale_book(a)
+        scale_book(0, 1)
+        scale_book(1, 2)
+        for a in range(1, 4):
+            scale_book(2 * a, 2 * a + 2)
         turn_book(0)
         turn_book(1)
-        warm(2)
         turn_book(2)
         turn_book(3)
         quantise_book(0)
@@ -258,21 +288,25 @@ def tile_codingclassifier_kernel(tc, output, code_book, out):
         sum_book(2)
         sum_book(3)
         keep_sums(1)
-        quantise(0)
         row_sum(0, 3)
+        quantise(0, 2)
+        fold_batch(1)
 
         for b in range(N_BATCH):
             more = b + 1 < N_BATCH
-            if more:
-                transposes(b + 1)
-                for s in range(S_PER):
-                    copy_out(b + 1, s)
+            turn_at = 2 if b == 0 else 0
             for s in range(S_PER):
+                if more and s == turn_at:
+                    transposes(b + 1)
+                    for z in range(S_PER):
+                        copy_out(b + 1, z)
                 accs = multiply(b, s)
                 if more and not on_vector(b + 1, s):
                     row_sum(b + 1, s)
                 finish(b, s, accs)
-                if more and s == 1:
+                if more and s == max(turn_at, 1):
                     quantise(b + 1)
+                    if b + 2 < N_BATCH:
+                        fold_batch(b + 2)
                 if more and on_vector(b + 1, s):
                     row_sum(b + 1, s)

@@ -43,8 +43,7 @@ def tile_codingclassifier_kernel(tc, output, code_book, out):
         spool = ctx.enter_context(tc.tile_pool(name="spool", bufs=16))
         jpool = ctx.enter_context(tc.tile_pool(name="jpool", bufs=1))
         fpool = ctx.enter_context(tc.tile_pool(name="fpool", bufs=6))
-        tpool = ctx.enter_context(tc.psum_pool(name="tpool", bufs=4))
-        apool = ctx.enter_context(tc.psum_pool(name="apool", bufs=4))
+        ppool = ctx.enter_context(tc.psum_pool(name="ppool", bufs=8))
 
         ident = const.tile([P, P], F32, name="ident")
         make_identity(nc, ident[:])
@@ -89,7 +88,7 @@ def tile_codingclassifier_kernel(tc, output, code_book, out):
             )
 
         def turn_book(t):
-            tp = tpool.tile([P, 4, P], F32, name="tp")
+            tp = ppool.tile([P, 4, P], F32, name="bank")
             for q in range(4):
                 nc.tensor.transpose(
                     out=tp[:, q, :],
@@ -112,7 +111,7 @@ def tile_codingclassifier_kernel(tc, output, code_book, out):
 
         def sum_book(a):
             if a % 2 == 0:
-                ccp = apool.tile([P, HALF], F32, name="acc")
+                ccp = ppool.tile([P, HALF], F32, name="bank")
                 ccps[a // 2] = ccp
             ccp = ccps[a // 2]
             for i in range(8):
@@ -137,7 +136,7 @@ def tile_codingclassifier_kernel(tc, output, code_book, out):
         def transposes(b):
             xw = x_tiles[b][:].bitcast(F32)
             for s in range(S_PER):
-                tp = tpool.tile([P, 4, P], F32, name="tp")
+                tp = ppool.tile([P, 4, P], F32, name="bank")
                 for q in range(4):
                     nc.tensor.transpose(
                         out=tp[:, q, :],
@@ -219,7 +218,7 @@ def tile_codingclassifier_kernel(tc, output, code_book, out):
             xc, xs = xq[b]
             accs = []
             for h in range(2):
-                acc = apool.tile([P, HALF], F32, name="acc")
+                acc = ppool.tile([P, HALF], F32, name="bank")
                 for g in range(2):
                     off = g * N_CODES + h * HALF
                     col = s * 256 + g * P
@@ -304,7 +303,7 @@ def tile_codingclassifier_kernel(tc, output, code_book, out):
                 if more and not on_vector(b + 1, s):
                     row_sum(b + 1, s)
                 finish(b, s, accs)
-                if more and s == max(turn_at, 1):
+                if more and s == 2:
                     quantise(b + 1)
                     if b + 2 < N_BATCH:
                         fold_batch(b + 2)

from contextlib import ExitStack

import concourse.mybir as mybir
from concourse.masks import make_identity

F32 = mybir.dt.float32
BF16 = mybir.dt.bfloat16
U32 = mybir.dt.uint32
U8 = mybir.dt.uint8
FP8X4 = mybir.dt.float8_e4m3fn_x4
ALU = mybir.AluOpType
ACT = mybir.ActivationFunctionType

P = 128
N_ROWS = 4096
C_LEN = 1024
N_CODES = 1024
FLOPS = 2 * N_ROWS * C_LEN * N_CODES

S_PER = 4
N_BATCH = N_ROWS // (P * S_PER)
JT = N_CODES // P
HALF = 512


def on_vector(b, s):
    return b == 0


def folded(b, s):
    return b > 0 and s < 3


def tile_codingclassifier_kernel(tc, output, code_book, out):
    nc = tc.nc
    with ExitStack() as ctx:
        ctx.enter_context(tc.manual_schedule())
        const = ctx.enter_context(tc.tile_pool(name="const", bufs=1))
        xin = ctx.enter_context(tc.tile_pool(name="xin", bufs=N_BATCH))
        gpool = ctx.enter_context(tc.tile_pool(name="gpool", bufs=3))
        qpool = ctx.enter_context(tc.tile_pool(name="qpool", bufs=3))
        rpool = ctx.enter_context(tc.tile_pool(name="rpool", bufs=6))
        spool = ctx.enter_context(tc.tile_pool(name="spool", bufs=16))
        jpool = ctx.enter_context(tc.tile_pool(name="jpool", bufs=1))
        fpool = ctx.enter_context(tc.tile_pool(name="fpool", bufs=6))
        ppool = ctx.enter_context(tc.psum_pool(name="ppool", bufs=8))

        ident = const.tile([P, P], F32, name="ident")
        make_identity(nc, ident[:])
        negh = const.tile([P, P], BF16, name="negh")
        nc.gpsimd.memset(negh[:], -0.5)

        cb_sb = const.tile([P, JT * C_LEN], BF16, name="cb_sb")
        cb_view = code_book.rearrange("(t p) c -> p t c", p=P)
        for t in range(2):
            nc.sync.dma_start(out=cb_sb[:, t * C_LEN : (t + 1) * C_LEN], in_=cb_view[:, t, :])
        for a in range(1, 4):
            nc.sync.dma_start(
                out=cb_sb[:, a * 2048 : (a + 1) * 2048].rearrange("p (t c) -> p t c", t=2),
                in_=cb_view[:, 2 * a : 2 * a + 2, :],
            )
        x_view = output.rearrange("(b p s) c -> b p (s c)", p=P, s=S_PER)
        o_view = out.rearrange("(b p s) j -> b p (s j)", p=P, s=S_PER)
        x_tiles = []
        for b in range(N_BATCH):
            x_sb = xin.tile([P, S_PER * C_LEN], BF16, name="x_sb")
            nc.sync.dma_start(out=x_sb[:], in_=x_view[b])
            x_tiles.append(x_sb)

        junk_s = jpool.tile([P, C_LEN], BF16, name="junk_s")
        junk_w = jpool.tile([P, HALF], F32, name="junk_w")

        cbz = const.tile([P, JT * C_LEN], BF16, name="cbz")
        cb_w = cbz[:].bitcast(F32)
        gcb = const.tile([P, 2 * N_CODES * 4], BF16, name="gcb", align_bytes=64)
        gcb_w = gcb[:].bitcast(F32).rearrange("p (g j u) -> p g j u", g=2, u=2)
        gcb_e = gcb[:].rearrange("p (g j e) -> p g j e", g=2, e=4)
        cbc = const.tile([P, 2 * N_CODES], U32, name="cbc", align_bytes=64)
        cbs = const.tile([P, 2 * N_CODES], U8, name="cbs", align_bytes=64)
        cc = const.tile([P, N_CODES], F32, name="cc")
        ccps = {}

        def scale_book(lo, hi):
            nc.vector.tensor_scalar(
                out=cbz[:, lo * C_LEN : hi * C_LEN],
                in0=cb_sb[:, lo * C_LEN : hi * C_LEN],
                scalar1=2.0 / 1024.0, scalar2=None, op0=ALU.mult,
            )

        def turn_book(t):
            tp = ppool.tile([P, 4, P], F32, name="bank")
            for q in range(4):
                nc.tensor.transpose(
                    out=tp[:, q, :],
                    in_=cb_w[:, t * 512 + q * P : t * 512 + (q + 1) * P],
                    identity=ident[:],
                )
            nc.scalar.copy(
                out=gcb_w[:, :, t * P : (t + 1) * P, :],
                in_=tp[:].rearrange("p (g u) r -> p g r u", g=2),
            )

        def quantise_book(hh):
            for g in range(2):
                off = g * N_CODES + hh * HALF
                nc.vector.quantize_mx(
                    out=cbc[:, off : off + HALF].bitcast(FP8X4),
                    scales=cbs[:, off : off + HALF],
                    in_=gcb[:, off * 4 : (off + HALF) * 4],
                )

        def sum_book(a):
            if a % 2 == 0:
                ccp = ppool.tile([P, HALF], F32, name="bank")
                ccps[a // 2] = ccp
            ccp = ccps[a // 2]
            for i in range(8):
                nc.tensor.matmul(
                    out=ccp[:, (a % 2) * 256 : (a % 2 + 1) * 256],
                    lhsT=negh[:],
                    rhs=gcb_e[:, i // 4, a * 256 : (a + 1) * 256, i % 4],
                    start=(i == 0),
                    stop=(i == 7),
                )

        def keep_sums(hh):
            nc.scalar.activation(
                out=cc[:, hh * HALF : (hh + 1) * HALF], in_=ccps[hh][:], func=ACT.Copy, bias=1.0, scale=1.0,
            )

        tps = {}
        grps = {}
        xq = {}
        noss = {}

        def transposes(b):
            xw = x_tiles[b][:].bitcast(F32)
            for s in range(S_PER):
                tp = ppool.tile([P, 4, P], F32, name="bank")
                for q in range(4):
                    nc.tensor.transpose(
                        out=tp[:, q, :],
                        in_=xw[:, s * 512 + q * P : s * 512 + (q + 1) * P],
                        identity=ident[:],
                    )
                tps[(b, s)] = tp

        def copy_out(b, s):
            if s == 0:
                grp = gpool.tile([P, S_PER * C_LEN], BF16, name="grp", align_bytes=64)
                grps[b] = grp
            nc.scalar.copy(
                out=grps[b][:, s * C_LEN : (s + 1) * C_LEN].bitcast(F32).rearrange("p (g r u) -> p g r u", g=2, u=2),
                in_=tps[(b, s)][:].rearrange("p (g u) r -> p g r u", g=2),
            )

        folds = {}
        gate = const.tile([P, 8], U32, name="gate")

        def fold_batch(b):
            nc.gpsimd.tensor_copy(out=gate[:], in_=xq[b - 1][0][:, 0:8])
            for s in range(S_PER):
                if folded(b, s):
                    lo = s * C_LEN
                    fo = fpool.tile([P, HALF], F32, name="fo")
                    nc.gpsimd.tensor_tensor(
                        out=fo[:], in0=x_tiles[b][:, lo : lo + HALF], in1=x_tiles[b][:, lo + HALF : lo + C_LEN], op=ALU.add,
                    )
                    folds[(b, s)] = fo
            xc = qpool.tile([P, S_PER * 256], U32, name="xc", align_bytes=64)
            xs = qpool.tile([P, S_PER * 256], U8, name="xs", align_bytes=64)
            nc.gpsimd.memset(xs[:, 0:64], 0)
            xq[b] = (xc, xs)

        def row_sum(b, s):
            nos = spool.tile([P, 1], F32, name="nos")
            lo = s * C_LEN
            if on_vector(b, s):
                raw = spool.tile([P, 1], F32, name="raw")
                nc.vector.scalar_tensor_tensor(
                    out=junk_w[:],
                    in0=x_tiles[b][:, lo : lo + HALF],
                    scalar=1.0,
                    in1=x_tiles[b][:, lo + HALF : lo + C_LEN],
                    op0=ALU.mult, op1=ALU.add, accum_out=raw[:],
                )
                nc.gpsimd.tensor_scalar(
                    out=nos[:], in0=raw[:], scalar1=-1.0 / 1024.0, scalar2=0.0, op0=ALU.mult, op1=ALU.add,
                )
            elif folded(b, s):
                nc.scalar.activation(
                    out=junk_s[:, 0:HALF], in_=folds[(b, s)][:], func=ACT.Copy,
                    scale=-1.0 / 1024.0, accum_out=nos[:],
                )
            else:
                nc.scalar.activation(
                    out=junk_s[:], in_=x_tiles[b][:, lo : lo + C_LEN], func=ACT.Copy,
                    scale=-1.0 / 1024.0, accum_out=nos[:],
                )
            noss[(b, s)] = nos

        def quantise(b, parts=1):
            if b == 0:
                xc = qpool.tile([P, S_PER * 256], U32, name="xc", align_bytes=64)
                xs = qpool.tile([P, S_PER * 256], U8, name="xs", align_bytes=64)
                xq[b] = (xc, xs)
            xc, xs = xq[b]
            w = S_PER * 256 // parts
            for i in range(parts):
                nc.vector.quantize_mx(
                    out=xc[:, i * w : (i + 1) * w].bitcast(FP8X4), scales=xs[:, i * w : (i + 1) * w],
                    in_=grps[b][:, i * w * 4 : (i + 1) * w * 4],
                )

        res_box = [None]

        def multiply(b, s):
            xc, xs = xq[b]
            accs = []
            for h in range(2):
                acc = ppool.tile([P, HALF], F32, name="bank")
                for g in range(2):
                    off = g * N_CODES + h * HALF
                    col = s * 256 + g * P
                    nc.tensor.matmul_mx(
                        out=acc[:],
                        lhsT=xc[:, col : col + P].bitcast(FP8X4),
                        lhsT_scale=xs[:, col : col + P],
                        rhs=cbc[:, off : off + HALF].bitcast(FP8X4),
                        rhs_scale=cbs[:, off : off + HALF],
                        start=(g == 0),
                        stop=(g == 1),
                    )
                accs.append(acc)
            return accs

        def finish(b, s, accs):
            fine = 0 if b < N_BATCH - 2 else (2 if (b == N_BATCH - 1 and s >= 2) else 1)
            if s % 2 == 0:
                res = rpool.tile([P, 2 * N_CODES], F32, name="res")
                res_box[0] = res
            res = res_box[0]
            for h in range(2):
                col = (s % 2) * N_CODES + h * HALF
                nc.vector.scalar_tensor_tensor(
                    out=res[:, col : col + HALF],
                    in0=accs[h][:],
                    scalar=noss[(b, s)][:],
                    in1=cc[:, h * HALF : (h + 1) * HALF],
                    op0=ALU.add,
                    op1=ALU.add,
                )
                if fine == 2:
                    lo = s * N_CODES + h * HALF
                    nc.sync.dma_start(out=o_view[b][:, lo : lo + HALF], in_=res[:, col : col + HALF])
            if fine == 1:
                lo = s * N_CODES
                col = (s % 2) * N_CODES
                nc.sync.dma_start(out=o_view[b][:, lo : lo + N_CODES], in_=res[:, col : col + N_CODES])
            if fine == 0 and s % 2 == 1:
                lo = (s - 1) * N_CODES
                nc.sync.dma_start(out=o_view[b][:, lo : lo + 2 * N_CODES], in_=res[:])

        scale_book(0, 1)
        scale_book(1, 2)
        for a in range(1, 4):
            scale_book(2 * a, 2 * a + 2)
        turn_book(0)
        turn_book(1)
        turn_book(2)
        turn_book(3)
        quantise_book(0)
        row_sum(0, 0)
        row_sum(0, 1)
        sum_book(0)
        turn_book(4)
        turn_book(5)
        sum_book(1)
        keep_sums(0)
        turn_book(6)
        turn_book(7)
        quantise_book(1)
        row_sum(0, 2)
        transposes(0)
        for s in range(S_PER):
            copy_out(0, s)
        sum_book(2)
        sum_book(3)
        keep_sums(1)
        row_sum(0, 3)
        quantise(0, 2)
        fold_batch(1)

        for b in range(N_BATCH):
            more = b + 1 < N_BATCH
            turn_at = 2 if b == 0 else 0
            for s in range(S_PER):
                if more and s == turn_at:
                    transposes(b + 1)
                    for z in range(S_PER):
                        copy_out(b + 1, z)
                accs = multiply(b, s)
                if more and not on_vector(b + 1, s):
                    row_sum(b + 1, s)
                finish(b, s, accs)
                if more and s == 2:
                    quantise(b + 1)
                    if b + 2 < N_BATCH:
                        fold_batch(b + 2)
                if more and on_vector(b + 1, s):
                    row_sum(b + 1, s)
